import numpy as np
import ml_dtypes


def mxq(x, axis, fmt="e4m3"):
    dtype, down = {"e4m3": (ml_dtypes.float8_e4m3fn, 7), "e5m2": (ml_dtypes.float8_e5m2, 14)}[fmt]
    v = np.moveaxis(np.asarray(x, np.float32).astype(ml_dtypes.bfloat16).astype(np.float64), axis, -1)
    blocks = v.reshape(v.shape[:-1] + (-1, 32))
    amax = np.abs(blocks).max(-1, keepdims=True)
    byte = np.maximum(np.where(amax > 0, np.frexp(amax)[1] - 1 + 127, 0) - down, 1)
    scale = np.exp2(byte - 127.0)
    codes = (blocks / scale).astype(np.float32).astype(dtype).astype(np.float64)
    return np.moveaxis((codes * scale).reshape(v.shape), -1, axis)


WIDE = False


def mx_kscale(k):
    if not WIDE:
        return np.ones(k)
    levels = np.array([10, -10, 5, -5, 0])
    a = np.random.permutation(np.resize(levels, k // 512 * 4)).reshape(k // 512, 4)
    idx = np.arange(k)
    return np.exp2(a[idx // 512, idx % 128 // 32])


BF16 = ml_dtypes.bfloat16


def bf(x):
    return np.asarray(x, np.float32).astype(BF16)


def f64(x):
    return np.asarray(x).astype(np.float64)


B, C, D, MIP, HH, WW = 8, 512, 256, 32, 32, 32
N = HH * WW


def sigmoid(v):
    return 1.0 / (1.0 + np.exp(-v))


def setup_inputs():
    s = mx_kscale(C)
    return {"x": bf(np.random.standard_normal((B, C, HH, WW)) * s[None, :, None, None]),
            "q_w": bf(np.random.standard_normal((D, C)) * 0.6 / np.sqrt(C) / s[None, :]),
            "q_b": bf(np.random.standard_normal(D) * 0.1),
            "k_w": bf(np.random.standard_normal((D, C)) * 0.6 / np.sqrt(C) / s[None, :]),
            "k_b": bf(np.random.standard_normal(D) * 0.1),
            "a_h": bf(sigmoid(np.random.standard_normal((B, D, HH))) / s[None, :D, None]),
            "a_w": bf(sigmoid(np.random.standard_normal((B, D, WW))))}


def reference(x, q_w, q_b, k_w, k_b, a_h, a_w):
    x4 = f64(x)
    xq = mxq(x4.reshape(B, C, N), 1, "e4m3")
    q = ((mxq(f64(q_w), 1, "e4m3") @ xq) + f64(q_b)[None, :, None]).transpose(0, 2, 1)
    k = (mxq(f64(k_w), 1, "e4m3") @ xq) + f64(k_b)[None, :, None]
    bias = (f64(a_w)[:, :, None, :] * f64(a_h)[:, :, :, None] * x4[:, :D]).reshape(B, D, N)
    return q, k + bias

@@ -1,0 +1,169 @@
+from contextlib import ExitStack
+
+import concourse.mybir as mybir
+from concourse.masks import make_identity
+
+F32 = mybir.dt.float32
+BF16 = mybir.dt.bfloat16
+U32 = mybir.dt.uint32
+U8 = mybir.dt.uint8
+FP8X4 = mybir.dt.float8_e4m3fn_x4
+ADD = mybir.AluOpType.add
+MULT = mybir.AluOpType.mult
+COPY = mybir.ActivationFunctionType.Copy
+
+B, C, D, HH, WW = 8, 512, 256, 32, 32
+N = HH * WW
+P = 128
+PACK = 4
+HALF = 512
+R = HALF // P
+
+FLOPS = 2 * 2 * B * D * C * N
+
+
+def quantise_weight(nc, const, psum, ident, rows, label):
+    turned = psum.tile([P, 2, D], F32, tag="bank", name=label + "_turned")
+    for h in range(2):
+        words = rows[:, h, :].bitcast(F32)
+        for u in range(2):
+            nc.tensor.transpose(turned[:, u, h * P : (h + 1) * P], words[:, u * P : (u + 1) * P], ident[:])
+    grouped = const.tile([P, D * PACK], BF16, align_bytes=64, name=label + "_grouped")
+    nc.vector.tensor_copy(
+        out=grouped[:].bitcast(F32).rearrange("p (c u) -> p c u", u=2),
+        in_=turned[:].rearrange("p u c -> p c u"),
+    )
+    codes = const.tile([P, D], U32, align_bytes=64, name=label + "_codes")
+    scales = const.tile([P, D], U8, align_bytes=64, name=label + "_scales")
+    nc.vector.quantize_mx(out=codes[:].bitcast(FP8X4), scales=scales[:], in_=grouped[:])
+    return codes, scales
+
+
+def tile_self_attn_pa_t_kernel(tc, x, q_w, q_b, k_w, k_b, a_h, a_w, out_0, out_1):
+    nc = tc.nc
+    with ExitStack() as ctx:
+        const = ctx.enter_context(tc.tile_pool(name="const", bufs=1))
+        maps = ctx.enter_context(tc.tile_pool(name="maps", bufs=B))
+        work = ctx.enter_context(tc.tile_pool(name="work", bufs=2))
+        results = ctx.enter_context(tc.tile_pool(name="results", bufs=3))
+        psum = ctx.enter_context(tc.psum_pool(name="psum", bufs=8))
+
+        kw_rows = const.tile([P, 2, C], BF16)
+        nc.sync.dma_start(out=kw_rows[:], in_=k_w.rearrange("(p e) c -> p e c", e=2))
+        qw_rows = const.tile([P, 2, C], BF16)
+        nc.sync.dma_start(out=qw_rows[:], in_=q_w.rearrange("(h p) c -> p h c", p=P))
+        x_tiles = []
+        for b in range(B):
+            x_b = maps.tile([P, PACK, N], BF16)
+            nc.sync.dma_start(
+                out=x_b[:].rearrange("p (u e) n -> p u (e n)", u=2),
+                in_=x[b].rearrange("(u p e) i j -> p u (e i j)", u=2, e=2),
+            )
+            x_tiles.append(x_b)
+
+        ah = const.tile([P, B, 2, HH], BF16)
+        nc.scalar.dma_start(
+            out=ah[:].rearrange("p b e i -> p b (e i)"), in_=a_h.rearrange("b (p e) i -> p b (e i)", e=2)
+        )
+        aw = const.tile([P, B, 2, WW], BF16)
+        nc.scalar.dma_start(
+            out=aw[:].rearrange("p b e j -> p b (e j)"), in_=a_w.rearrange("b (p e) j -> p b (e j)", e=2)
+        )
+        kb_bf = const.tile([P, 2], BF16)
+        nc.scalar.dma_start(out=kb_bf[:], in_=k_b.rearrange("(p e) -> p e", e=2))
+        qb_bf = const.tile([P, D], BF16)
+        nc.scalar.dma_start(out=qb_bf[:], in_=q_b.partition_broadcast(P))
+
+        ident = const.tile([P, P], F32)
+        make_identity(nc, ident[:])
+        kw_codes, kw_scales = quantise_weight(nc, const, psum, ident, kw_rows, "kw")
+        qw_codes, qw_scales = quantise_weight(nc, const, psum, ident, qw_rows, "qw")
+        ah_f32 = const.tile([P, B, 2, HH], F32)
+        nc.vector.tensor_copy(out=ah_f32[:], in_=ah[:])
+        kb = const.tile([P, 2], F32)
+        nc.vector.tensor_copy(out=kb[:], in_=kb_bf[:])
+        qb = const.tile([P, 2, D], F32)
+        nc.vector.tensor_copy(out=qb[:], in_=qb_bf[:].unsqueeze(1).to_broadcast([P, 2, D]))
+
+        for b in range(B):
+            x_b = x_tiles[b]
+
+            gated_even = work.tile([P, N], F32)
+            for i in range(HH):
+                nc.scalar.activation(
+                    out=gated_even[:, i * WW : (i + 1) * WW], in_=aw[:, b, 0, :], func=COPY, scale=ah_f32[:, b, 0, i : i + 1]
+                )
+            gated_odd = work.tile([P, N], F32)
+            nc.gpsimd.tensor_tensor(
+                out=gated_odd[:].rearrange("p (i j) -> p i j", j=WW),
+                in0=ah[:, b, 1, :].unsqueeze(2).to_broadcast([P, HH, WW]),
+                in1=aw[:, b, 1, :].unsqueeze(1).to_broadcast([P, HH, WW]),
+                op=MULT,
+            )
+            nc.gpsimd.tensor_tensor(out=gated_odd[:], in0=gated_odd[:], in1=x_b[:, 1, :], op=MULT)
+            gated = [gated_even, gated_odd]
+
+            grouped = work.tile([P, 2, R, P, PACK], BF16, align_bytes=64)
+            codes = work.tile([P, N], U32, align_bytes=64)
+            scales = work.tile([P, N], U8, align_bytes=64)
+            q_sb = results.tile([P, 2, R, D], F32)
+            k_sb = results.tile([P, 2, N], F32)
+
+            for g in range(2):
+                pixels = slice(g * HALF, (g + 1) * HALF)
+                nc.scalar.copy(
+                    out=grouped[:, g], in_=x_b[:, :, pixels].rearrange("p t (m r) -> p r m t", r=R)
+                )
+                nc.vector.quantize_mx(
+                    out=codes[:, pixels].bitcast(FP8X4),
+                    scales=scales[:, pixels],
+                    in_=grouped[:, g].rearrange("p r m t -> p (r m t)"),
+                )
+                nc.vector.tensor_tensor(
+                    out=gated_even[:, pixels], in0=gated_even[:, pixels], in1=x_b[:, 0, pixels], op=MULT
+                )
+
+                for e in range(2):
+                    k_acc = psum.tile([P, HALF], F32, tag="bank")
+                    nc.tensor.matmul_mx(
+                        out=k_acc[:],
+                        lhsT=kw_codes[:, e * P : (e + 1) * P].bitcast(FP8X4),
+                        lhsT_scale=kw_scales[:, e * P : (e + 1) * P],
+                        rhs=codes[:, pixels].bitcast(FP8X4),
+                        rhs_scale=scales[:, pixels],
+                        start=True,
+                        stop=True,
+                    )
+                    nc.vector.scalar_tensor_tensor(
+                        out=k_sb[:, e, pixels].rearrange("p (m r) -> p m r", r=R),
+                        in0=k_acc[:].rearrange("p (r m) -> p m r", r=R),
+                        scalar=kb[:, e : e + 1],
+                        in1=gated[e][:, pixels].rearrange("p (m r) -> p m r", r=R),
+                        op0=ADD,
+                        op1=ADD,
+                    )
+
+                for pair in range(R // 2):
+                    q_acc = psum.tile([P, 2, D], F32, tag="bank")
+                    for s in range(2):
+                        first = g * HALF + (2 * pair + s) * P
+                        nc.tensor.matmul_mx(
+                            out=q_acc[:, s, :],
+                            lhsT=codes[:, first : first + P].bitcast(FP8X4),
+                            lhsT_scale=scales[:, first : first + P],
+                            rhs=qw_codes[:].bitcast(FP8X4),
+                            rhs_scale=qw_scales[:],
+                            start=True,
+                            stop=True,
+                        )
+                    nc.vector.tensor_tensor(
+                        out=q_sb[:, g, 2 * pair : 2 * pair + 2, :], in0=q_acc[:], in1=qb[:], op=ADD
+                    )
+
+                nc.sync.dma_start(
+                    out=out_1[b].rearrange("(p e) n -> p e n", e=2)[:, :, pixels], in_=k_sb[:, :, pixels]
+                )
+                nc.sync.dma_start(
+                    out=out_0[b, pixels, :].rearrange("(m r) d -> m (r d)", r=R),
+                    in_=q_sb[:, g].rearrange("m r d -> m (r d)"),
+                )

@@ -17,7 +17,8 @@ N = HH * WW
 P = 128
 PACK = 4
 HALF = 512
-R = HALF // P
+Q_TILES = HALF // P
+RUN = 4
 
 FLOPS = 2 * 2 * B * D * C * N
 
@@ -103,21 +104,22 @@ def tile_self_attn_pa_t_kernel(tc, x, q_w, q_b, k_w, k_b, a_h, a_w, out_0, out_1
             nc.gpsimd.tensor_tensor(out=gated_odd[:], in0=gated_odd[:], in1=x_b[:, 1, :], op=MULT)
             gated = [gated_even, gated_odd]
 
-            grouped = work.tile([P, 2, R, P, PACK], BF16, align_bytes=64)
+            grouped = work.tile([P, 2, HALF, PACK], BF16, align_bytes=64)
             codes = work.tile([P, N], U32, align_bytes=64)
             scales = work.tile([P, N], U8, align_bytes=64)
-            q_sb = results.tile([P, 2, R, D], F32)
+            q_sb = results.tile([P, 2, Q_TILES, D], F32)
             k_sb = results.tile([P, 2, N], F32)
 
             for g in range(2):
                 pixels = slice(g * HALF, (g + 1) * HALF)
                 nc.scalar.copy(
-                    out=grouped[:, g], in_=x_b[:, :, pixels].rearrange("p t (m r) -> p r m t", r=R)
+                    out=grouped[:, g].rearrange("p (c i) t -> p c t i", i=RUN),
+                    in_=x_b[:, :, pixels].rearrange("p t (c i) -> p c t i", i=RUN),
                 )
                 nc.vector.quantize_mx(
                     out=codes[:, pixels].bitcast(FP8X4),
                     scales=scales[:, pixels],
-                    in_=grouped[:, g].rearrange("p r m t -> p (r m t)"),
+                    in_=grouped[:, g].rearrange("p n t -> p (n t)"),
                 )
                 nc.vector.tensor_tensor(
                     out=gated_even[:, pixels], in0=gated_even[:, pixels], in1=x_b[:, 0, pixels], op=MULT
@@ -135,15 +137,15 @@ def tile_self_attn_pa_t_kernel(tc, x, q_w, q_b, k_w, k_b, a_h, a_w, out_0, out_1
                         stop=True,
                     )
                     nc.vector.scalar_tensor_tensor(
-                        out=k_sb[:, e, pixels].rearrange("p (m r) -> p m r", r=R),
-                        in0=k_acc[:].rearrange("p (r m) -> p m r", r=R),
+                        out=k_sb[:, e, pixels],
+                        in0=k_acc[:],
                         scalar=kb[:, e : e + 1],
-                        in1=gated[e][:, pixels].rearrange("p (m r) -> p m r", r=R),
+                        in1=gated[e][:, pixels],
                         op0=ADD,
                         op1=ADD,
                     )
 
-                for pair in range(R // 2):
+                for pair in range(Q_TILES // 2):
                     q_acc = psum.tile([P, 2, D], F32, tag="bank")
                     for s in range(2):
                         first = g * HALF + (2 * pair + s) * P
@@ -164,6 +166,6 @@ def tile_self_attn_pa_t_kernel(tc, x, q_w, q_b, k_w, k_b, a_h, a_w, out_0, out_1
                     out=out_1[b].rearrange("(p e) n -> p e n", e=2)[:, :, pixels], in_=k_sb[:, :, pixels]
                 )
                 nc.sync.dma_start(
-                    out=out_0[b, pixels, :].rearrange("(m r) d -> m (r d)", r=R),
-                    in_=q_sb[:, g].rearrange("m r d -> m (r d)"),
+                    out=out_0[b, pixels, :].rearrange("(s m) d -> m s d", m=P),
+                    in_=q_sb[:, g],
                 )

@@ -19,6 +19,7 @@ PACK = 4
 HALF = 512
 Q_TILES = HALF // P
 RUN = 4
+HALVES = N // HALF
 
 FLOPS = 2 * 2 * B * D * C * N
 
@@ -46,21 +47,26 @@ def tile_self_attn_pa_t_kernel(tc, x, q_w, q_b, k_w, k_b, a_h, a_w, out_0, out_1
         const = ctx.enter_context(tc.tile_pool(name="const", bufs=1))
         maps = ctx.enter_context(tc.tile_pool(name="maps", bufs=B))
         work = ctx.enter_context(tc.tile_pool(name="work", bufs=2))
+        gates = ctx.enter_context(tc.tile_pool(name="gates", bufs=3))
         results = ctx.enter_context(tc.tile_pool(name="results", bufs=3))
         psum = ctx.enter_context(tc.psum_pool(name="psum", bufs=8))
+        ctx.enter_context(tc.manual_schedule())
 
+        x_tiles = [maps.tile([P, PACK, N], BF16, name="x_b") for b in range(B)]
+
+        def load_map(b):
+            nc.sync.dma_start(
+                out=x_tiles[b][:].rearrange("p (u e) n -> p u (e n)", u=2),
+                in_=x[b].rearrange("(u p e) i j -> p u (e i j)", u=2, e=2),
+            )
+
+        load_map(0)
         kw_rows = const.tile([P, 2, C], BF16)
         nc.sync.dma_start(out=kw_rows[:], in_=k_w.rearrange("(p e) c -> p e c", e=2))
         qw_rows = const.tile([P, 2, C], BF16)
         nc.sync.dma_start(out=qw_rows[:], in_=q_w.rearrange("(h p) c -> p h c", p=P))
-        x_tiles = []
-        for b in range(B):
-            x_b = maps.tile([P, PACK, N], BF16)
-            nc.sync.dma_start(
-                out=x_b[:].rearrange("p (u e) n -> p u (e n)", u=2),
-                in_=x[b].rearrange("(u p e) i j -> p u (e i j)", u=2, e=2),
-            )
-            x_tiles.append(x_b)
+        for b in range(1, B):
+            load_map(b)
 
         ah = const.tile([P, B, 2, HH], BF16)
         nc.scalar.dma_start(
@@ -77,95 +83,123 @@ def tile_self_attn_pa_t_kernel(tc, x, q_w, q_b, k_w, k_b, a_h, a_w, out_0, out_1
 
         ident = const.tile([P, P], F32)
         make_identity(nc, ident[:])
-        kw_codes, kw_scales = quantise_weight(nc, const, psum, ident, kw_rows, "kw")
-        qw_codes, qw_scales = quantise_weight(nc, const, psum, ident, qw_rows, "qw")
         ah_f32 = const.tile([P, B, 2, HH], F32)
         nc.vector.tensor_copy(out=ah_f32[:], in_=ah[:])
+        kw_codes, kw_scales = quantise_weight(nc, const, psum, ident, kw_rows, "kw")
+        qw_codes, qw_scales = quantise_weight(nc, const, psum, ident, qw_rows, "qw")
         kb = const.tile([P, 2], F32)
         nc.vector.tensor_copy(out=kb[:], in_=kb_bf[:])
         qb = const.tile([P, 2, D], F32)
         nc.vector.tensor_copy(out=qb[:], in_=qb_bf[:].unsqueeze(1).to_broadcast([P, 2, D]))
 
-        for b in range(B):
-            x_b = x_tiles[b]
+        grouped, gated, codes, scales, banks, q_sb, k_sb = {}, {}, {}, {}, {}, {}, {}
 
-            gated_even = work.tile([P, N], F32)
+        def prepare(b):
+            x_b = x_tiles[b]
+            gated_even = gates.tile([P, N], F32)
             for i in range(HH):
                 nc.scalar.activation(
                     out=gated_even[:, i * WW : (i + 1) * WW], in_=aw[:, b, 0, :], func=COPY, scale=ah_f32[:, b, 0, i : i + 1]
                 )
-            gated_odd = work.tile([P, N], F32)
-            nc.gpsimd.tensor_tensor(
-                out=gated_odd[:].rearrange("p (i j) -> p i j", j=WW),
-                in0=ah[:, b, 1, :].unsqueeze(2).to_broadcast([P, HH, WW]),
-                in1=aw[:, b, 1, :].unsqueeze(1).to_broadcast([P, HH, WW]),
-                op=MULT,
-            )
-            nc.gpsimd.tensor_tensor(out=gated_odd[:], in0=gated_odd[:], in1=x_b[:, 1, :], op=MULT)
-            gated = [gated_even, gated_odd]
-
-            grouped = work.tile([P, 2, HALF, PACK], BF16, align_bytes=64)
-            codes = work.tile([P, N], U32, align_bytes=64)
-            scales = work.tile([P, N], U8, align_bytes=64)
-            q_sb = results.tile([P, 2, Q_TILES, D], F32)
-            k_sb = results.tile([P, 2, N], F32)
-
-            for g in range(2):
+            gated_odd = gates.tile([P, N], F32)
+            rows = HH // HALVES
+            for g in range(HALVES):
+                nc.gpsimd.tensor_tensor(
+                    out=gated_odd[:, g * HALF : (g + 1) * HALF].rearrange("p (i j) -> p i j", j=WW),
+                    in0=ah[:, b, 1, g * rows : (g + 1) * rows].unsqueeze(2).to_broadcast([P, rows, WW]),
+                    in1=aw[:, b, 1, :].unsqueeze(1).to_broadcast([P, rows, WW]),
+                    op=MULT,
+                )
+            for g in range(HALVES):
                 pixels = slice(g * HALF, (g + 1) * HALF)
+                nc.gpsimd.tensor_tensor(
+                    out=gated_odd[:, pixels], in0=gated_odd[:, pixels], in1=x_b[:, 1, pixels], op=MULT
+                )
+            gated[b] = [gated_even, gated_odd]
+            grouped[b] = work.tile([P, HALVES, HALF, PACK], BF16, align_bytes=64, name="grouped")
+            for g in range(HALVES):
                 nc.scalar.copy(
-                    out=grouped[:, g].rearrange("p (c i) t -> p c t i", i=RUN),
-                    in_=x_b[:, :, pixels].rearrange("p t (c i) -> p c t i", i=RUN),
-                )
-                nc.vector.quantize_mx(
-                    out=codes[:, pixels].bitcast(FP8X4),
-                    scales=scales[:, pixels],
-                    in_=grouped[:, g].rearrange("p n t -> p (n t)"),
-                )
-                nc.vector.tensor_tensor(
-                    out=gated_even[:, pixels], in0=gated_even[:, pixels], in1=x_b[:, 0, pixels], op=MULT
+                    out=grouped[b][:, g].rearrange("p (c i) t -> p c t i", i=RUN),
+                    in_=x_b[:, :, g * HALF : (g + 1) * HALF].rearrange("p t (c i) -> p c t i", i=RUN),
                 )
 
-                for e in range(2):
-                    k_acc = psum.tile([P, HALF], F32, tag="bank")
+        def quantise(b):
+            codes[b] = work.tile([P, N], U32, align_bytes=64, name="codes")
+            scales[b] = work.tile([P, N], U8, align_bytes=64, name="scales")
+            for g in range(HALVES):
+                pixels = slice(g * HALF, (g + 1) * HALF)
+                nc.vector.quantize_mx(
+                    out=codes[b][:, pixels].bitcast(FP8X4),
+                    scales=scales[b][:, pixels],
+                    in_=grouped[b][:, g].rearrange("p n t -> p (n t)"),
+                )
+            gated_even = gated[b][0]
+            nc.vector.tensor_tensor(out=gated_even[:], in0=gated_even[:], in1=x_tiles[b][:, 0, :], op=MULT)
+
+        def project(b, g):
+            pixels = slice(g * HALF, (g + 1) * HALF)
+            banks[b, g] = []
+            for e in range(2):
+                k_acc = psum.tile([P, HALF], F32, tag="bank")
+                nc.tensor.matmul_mx(
+                    out=k_acc[:],
+                    lhsT=kw_codes[:, e * P : (e + 1) * P].bitcast(FP8X4),
+                    lhsT_scale=kw_scales[:, e * P : (e + 1) * P],
+                    rhs=codes[b][:, pixels].bitcast(FP8X4),
+                    rhs_scale=scales[b][:, pixels],
+                    start=True,
+                    stop=True,
+                )
+                banks[b, g].append(k_acc)
+            for pair in range(Q_TILES // 2):
+                q_acc = psum.tile([P, 2, D], F32, tag="bank")
+                for s in range(2):
+                    first = g * HALF + (2 * pair + s) * P
                     nc.tensor.matmul_mx(
-                        out=k_acc[:],
-                        lhsT=kw_codes[:, e * P : (e + 1) * P].bitcast(FP8X4),
-                        lhsT_scale=kw_scales[:, e * P : (e + 1) * P],
-                        rhs=codes[:, pixels].bitcast(FP8X4),
-                        rhs_scale=scales[:, pixels],
+                        out=q_acc[:, s, :],
+                        lhsT=codes[b][:, first : first + P].bitcast(FP8X4),
+                        lhsT_scale=scales[b][:, first : first + P],
+                        rhs=qw_codes[:].bitcast(FP8X4),
+                        rhs_scale=qw_scales[:],
                         start=True,
                         stop=True,
                     )
-                    nc.vector.scalar_tensor_tensor(
-                        out=k_sb[:, e, pixels],
-                        in0=k_acc[:],
-                        scalar=kb[:, e : e + 1],
-                        in1=gated[e][:, pixels],
-                        op0=ADD,
-                        op1=ADD,
-                    )
+                banks[b, g].append(q_acc)
 
-                for pair in range(Q_TILES // 2):
-                    q_acc = psum.tile([P, 2, D], F32, tag="bank")
-                    for s in range(2):
-                        first = g * HALF + (2 * pair + s) * P
-                        nc.tensor.matmul_mx(
-                            out=q_acc[:, s, :],
-                            lhsT=codes[:, first : first + P].bitcast(FP8X4),
-                            lhsT_scale=scales[:, first : first + P],
-                            rhs=qw_codes[:].bitcast(FP8X4),
-                            rhs_scale=qw_scales[:],
-                            start=True,
-                            stop=True,
-                        )
-                    nc.vector.tensor_tensor(
-                        out=q_sb[:, g, 2 * pair : 2 * pair + 2, :], in0=q_acc[:], in1=qb[:], op=ADD
-                    )
+        def finish(b, g):
+            pixels = slice(g * HALF, (g + 1) * HALF)
+            if g == 0:
+                q_sb[b] = results.tile([P, HALVES, Q_TILES, D], F32, name="q_sb")
+                k_sb[b] = results.tile([P, 2, N], F32, name="k_sb")
+            for e in range(2):
+                nc.vector.scalar_tensor_tensor(
+                    out=k_sb[b][:, e, pixels],
+                    in0=banks[b, g][e][:],
+                    scalar=kb[:, e : e + 1],
+                    in1=gated[b][e][:, pixels],
+                    op0=ADD,
+                    op1=ADD,
+                )
+            nc.sync.dma_start(
+                out=out_1[b].rearrange("(p e) n -> p e n", e=2)[:, :, pixels], in_=k_sb[b][:, :, pixels]
+            )
+            for pair in range(Q_TILES // 2):
+                nc.vector.tensor_tensor(
+                    out=q_sb[b][:, g, 2 * pair : 2 * pair + 2, :], in0=banks[b, g][2 + pair][:], in1=qb[:], op=ADD
+                )
+            nc.sync.dma_start(out=out_0[b, pixels, :].rearrange("(s m) d -> m s d", m=P), in_=q_sb[b][:, g])
 
-                nc.sync.dma_start(
-                    out=out_1[b].rearrange("(p e) n -> p e n", e=2)[:, :, pixels], in_=k_sb[:, :, pixels]
-                )
-                nc.sync.dma_start(
-                    out=out_0[b, pixels, :].rearrange("(s m) d -> m s d", m=P),
-                    in_=q_sb[:, g],
-                )
+        prepare(0)
+        prepare(1)
+        quantise(0)
+        for g in range(HALVES):
+            project(0, g)
+        for b in range(B):
+            if b + 2 < B:
+                prepare(b + 2)
+            if b + 1 < B:
+                quantise(b + 1)
+            for g in range(HALVES):
+                finish(b, g)
+                if b + 1 < B:
+                    project(b + 1, g)

@@ -60,6 +60,14 @@ def tile_self_attn_pa_t_kernel(tc, x, q_w, q_b, k_w, k_b, a_h, a_w, out_0, out_1
                 in_=x[b].rearrange("(u p e) i j -> p u (e i j)", u=2, e=2),
             )
 
+        ah = const.tile([P, B, 2, HH], BF16)
+        nc.sync.dma_start(
+            out=ah[:].rearrange("p b e i -> p b (e i)"), in_=a_h.rearrange("b (p e) i -> p b (e i)", e=2)
+        )
+        aw = const.tile([P, B, 2, WW], BF16)
+        nc.sync.dma_start(
+            out=aw[:].rearrange("p b e j -> p b (e j)"), in_=a_w.rearrange("b (p e) j -> p b (e j)", e=2)
+        )
         load_map(0)
         kw_rows = const.tile([P, 2, C], BF16)
         nc.sync.dma_start(out=kw_rows[:], in_=k_w.rearrange("(p e) c -> p e c", e=2))
@@ -68,14 +76,6 @@ def tile_self_attn_pa_t_kernel(tc, x, q_w, q_b, k_w, k_b, a_h, a_w, out_0, out_1
         for b in range(1, B):
             load_map(b)
 
-        ah = const.tile([P, B, 2, HH], BF16)
-        nc.scalar.dma_start(
-            out=ah[:].rearrange("p b e i -> p b (e i)"), in_=a_h.rearrange("b (p e) i -> p b (e i)", e=2)
-        )
-        aw = const.tile([P, B, 2, WW], BF16)
-        nc.scalar.dma_start(
-            out=aw[:].rearrange("p b e j -> p b (e j)"), in_=a_w.rearrange("b (p e) j -> p b (e j)", e=2)
-        )
         kb_bf = const.tile([P, 2], BF16)
         nc.scalar.dma_start(out=kb_bf[:], in_=k_b.rearrange("(p e) -> p e", e=2))
         qb_bf = const.tile([P, D], BF16)
@@ -87,10 +87,6 @@ def tile_self_attn_pa_t_kernel(tc, x, q_w, q_b, k_w, k_b, a_h, a_w, out_0, out_1
         nc.vector.tensor_copy(out=ah_f32[:], in_=ah[:])
         kw_codes, kw_scales = quantise_weight(nc, const, psum, ident, kw_rows, "kw")
         qw_codes, qw_scales = quantise_weight(nc, const, psum, ident, qw_rows, "qw")
-        kb = const.tile([P, 2], F32)
-        nc.vector.tensor_copy(out=kb[:], in_=kb_bf[:])
-        qb = const.tile([P, 2, D], F32)
-        nc.vector.tensor_copy(out=qb[:], in_=qb_bf[:].unsqueeze(1).to_broadcast([P, 2, D]))
 
         grouped, gated, codes, scales, banks, q_sb, k_sb = {}, {}, {}, {}, {}, {}, {}
 
@@ -102,19 +98,13 @@ def tile_self_attn_pa_t_kernel(tc, x, q_w, q_b, k_w, k_b, a_h, a_w, out_0, out_1
                     out=gated_even[:, i * WW : (i + 1) * WW], in_=aw[:, b, 0, :], func=COPY, scale=ah_f32[:, b, 0, i : i + 1]
                 )
             gated_odd = gates.tile([P, N], F32)
-            rows = HH // HALVES
-            for g in range(HALVES):
-                nc.gpsimd.tensor_tensor(
-                    out=gated_odd[:, g * HALF : (g + 1) * HALF].rearrange("p (i j) -> p i j", j=WW),
-                    in0=ah[:, b, 1, g * rows : (g + 1) * rows].unsqueeze(2).to_broadcast([P, rows, WW]),
-                    in1=aw[:, b, 1, :].unsqueeze(1).to_broadcast([P, rows, WW]),
-                    op=MULT,
-                )
-            for g in range(HALVES):
-                pixels = slice(g * HALF, (g + 1) * HALF)
-                nc.gpsimd.tensor_tensor(
-                    out=gated_odd[:, pixels], in0=gated_odd[:, pixels], in1=x_b[:, 1, pixels], op=MULT
-                )
+            nc.gpsimd.tensor_tensor(
+                out=gated_odd[:].rearrange("p (i j) -> p i j", j=WW),
+                in0=ah[:, b, 1, :].unsqueeze(2).to_broadcast([P, HH, WW]),
+                in1=aw[:, b, 1, :].unsqueeze(1).to_broadcast([P, HH, WW]),
+                op=MULT,
+            )
+            nc.gpsimd.tensor_tensor(out=gated_odd[:], in0=gated_odd[:], in1=x_b[:, 1, :], op=MULT)
             gated[b] = [gated_even, gated_odd]
             grouped[b] = work.tile([P, HALVES, HALF, PACK], BF16, align_bytes=64, name="grouped")
             for g in range(HALVES):
@@ -126,6 +116,7 @@ def tile_self_attn_pa_t_kernel(tc, x, q_w, q_b, k_w, k_b, a_h, a_w, out_0, out_1
         def quantise(b):
             codes[b] = work.tile([P, N], U32, align_bytes=64, name="codes")
             scales[b] = work.tile([P, N], U8, align_bytes=64, name="scales")
+            gated_even = gated[b][0]
             for g in range(HALVES):
                 pixels = slice(g * HALF, (g + 1) * HALF)
                 nc.vector.quantize_mx(
@@ -133,8 +124,9 @@ def tile_self_attn_pa_t_kernel(tc, x, q_w, q_b, k_w, k_b, a_h, a_w, out_0, out_1
                     scales=scales[b][:, pixels],
                     in_=grouped[b][:, g].rearrange("p n t -> p (n t)"),
                 )
-            gated_even = gated[b][0]
-            nc.vector.tensor_tensor(out=gated_even[:], in0=gated_even[:], in1=x_tiles[b][:, 0, :], op=MULT)
+                nc.vector.tensor_tensor(
+                    out=gated_even[:, pixels], in0=gated_even[:, pixels], in1=x_tiles[b][:, 0, pixels], op=MULT
+                )
 
         def project(b, g):
             pixels = slice(g * HALF, (g + 1) * HALF)
@@ -194,6 +186,10 @@ def tile_self_attn_pa_t_kernel(tc, x, q_w, q_b, k_w, k_b, a_h, a_w, out_0, out_1
         quantise(0)
         for g in range(HALVES):
             project(0, g)
+        kb = const.tile([P, 2], F32)
+        nc.vector.tensor_copy(out=kb[:], in_=kb_bf[:])
+        qb = const.tile([P, 2, D], F32)
+        nc.vector.tensor_copy(out=qb[:], in_=qb_bf[:].unsqueeze(1).to_broadcast([P, 2, D]))
         for b in range(B):
             if b + 2 < B:
                 prepare(b + 2)

@@ -20,6 +20,7 @@ HALF = 512
 Q_TILES = HALF // P
 RUN = 4
 HALVES = N // HALF
+SCALAR_PIXELS = 3 * N // 4
 
 FLOPS = 2 * 2 * B * D * C * N
 
@@ -76,57 +77,62 @@ def tile_self_attn_pa_t_kernel(tc, x, q_w, q_b, k_w, k_b, a_h, a_w, out_0, out_1
         for b in range(1, B):
             load_map(b)
 
-        kb_bf = const.tile([P, 2], BF16)
-        nc.scalar.dma_start(out=kb_bf[:], in_=k_b.rearrange("(p e) -> p e", e=2))
-        qb_bf = const.tile([P, D], BF16)
-        nc.scalar.dma_start(out=qb_bf[:], in_=q_b.partition_broadcast(P))
+        kb = const.tile([P, 2], BF16)
+        nc.scalar.dma_start(out=kb[:], in_=k_b.rearrange("(p e) -> p e", e=2))
+        qb = const.tile([P, D], BF16)
+        nc.scalar.dma_start(out=qb[:], in_=q_b.partition_broadcast(P))
 
         ident = const.tile([P, P], F32)
         make_identity(nc, ident[:])
         ah_f32 = const.tile([P, B, 2, HH], F32)
         nc.vector.tensor_copy(out=ah_f32[:], in_=ah[:])
-        kw_codes, kw_scales = quantise_weight(nc, const, psum, ident, kw_rows, "kw")
-        qw_codes, qw_scales = quantise_weight(nc, const, psum, ident, qw_rows, "qw")
 
         grouped, gated, codes, scales, banks, q_sb, k_sb = {}, {}, {}, {}, {}, {}, {}
 
-        def prepare(b):
-            x_b = x_tiles[b]
-            gated_even = gates.tile([P, N], F32)
-            for i in range(HH):
-                nc.scalar.activation(
-                    out=gated_even[:, i * WW : (i + 1) * WW], in_=aw[:, b, 0, :], func=COPY, scale=ah_f32[:, b, 0, i : i + 1]
-                )
-            gated_odd = gates.tile([P, N], F32)
-            nc.gpsimd.tensor_tensor(
-                out=gated_odd[:].rearrange("p (i j) -> p i j", j=WW),
-                in0=ah[:, b, 1, :].unsqueeze(2).to_broadcast([P, HH, WW]),
-                in1=aw[:, b, 1, :].unsqueeze(1).to_broadcast([P, HH, WW]),
+        def gate_at_once(b):
+            gated[b] = gates.tile([P, 2, N], F32, name="gated")
+            nc.vector.tensor_tensor(
+                out=gated[b][:].rearrange("p e (i j) -> p e i j", j=WW),
+                in0=ah[:, b].unsqueeze(3).to_broadcast([P, 2, HH, WW]),
+                in1=aw[:, b].unsqueeze(2).to_broadcast([P, 2, HH, WW]),
                 op=MULT,
             )
-            nc.gpsimd.tensor_tensor(out=gated_odd[:], in0=gated_odd[:], in1=x_b[:, 1, :], op=MULT)
-            gated[b] = [gated_even, gated_odd]
-            grouped[b] = work.tile([P, HALVES, HALF, PACK], BF16, align_bytes=64, name="grouped")
+
+        def gate_by_rows(b):
+            gated[b] = gates.tile([P, 2, N], F32, name="gated")
+            for e in range(2):
+                for i in range(HH):
+                    nc.scalar.activation(
+                        out=gated[b][:, e, i * WW : (i + 1) * WW],
+                        in_=aw[:, b, e, :],
+                        func=COPY,
+                        scale=ah_f32[:, b, e, i : i + 1],
+                    )
+
+        def prepare(b):
+            x_b = x_tiles[b]
             for g in range(HALVES):
-                nc.scalar.copy(
-                    out=grouped[b][:, g].rearrange("p (c i) t -> p c t i", i=RUN),
-                    in_=x_b[:, :, g * HALF : (g + 1) * HALF].rearrange("p t (c i) -> p c t i", i=RUN),
-                )
+                pixels = slice(g * HALF, (g + 1) * HALF)
+                for e in range(2):
+                    nc.gpsimd.tensor_tensor(
+                        out=gated[b][:, e, pixels], in0=gated[b][:, e, pixels], in1=x_b[:, e, pixels], op=MULT
+                    )
+            grouped[b] = work.tile([P, N, PACK], BF16, align_bytes=64, name="grouped")
+            nc.scalar.copy(
+                out=grouped[b][:, :SCALAR_PIXELS].rearrange("p (c i) t -> p c t i", i=RUN),
+                in_=x_b[:, :, :SCALAR_PIXELS].rearrange("p t (c i) -> p c t i", i=RUN),
+            )
+            nc.vector.tensor_copy(
+                out=grouped[b][:, SCALAR_PIXELS:].rearrange("p (c i) t -> p c t i", i=RUN),
+                in_=x_b[:, :, SCALAR_PIXELS:].rearrange("p t (c i) -> p c t i", i=RUN),
+            )
 
         def quantise(b):
             codes[b] = work.tile([P, N], U32, align_bytes=64, name="codes")
             scales[b] = work.tile([P, N], U8, align_bytes=64, name="scales")
-            gated_even = gated[b][0]
-            for g in range(HALVES):
-                pixels = slice(g * HALF, (g + 1) * HALF)
-                nc.vector.quantize_mx(
-                    out=codes[b][:, pixels].bitcast(FP8X4),
-                    scales=scales[b][:, pixels],
-                    in_=grouped[b][:, g].rearrange("p n t -> p (n t)"),
-                )
-                nc.vector.tensor_tensor(
-                    out=gated_even[:, pixels], in0=gated_even[:, pixels], in1=x_tiles[b][:, 0, pixels], op=MULT
-                )
+            nc.vector.quantize_mx(
+                out=codes[b][:].bitcast(FP8X4), scales=scales[b][:], in_=grouped[b][:].rearrange("p n t -> p (n t)")
+            )
 
         def project(b, g):
             pixels = slice(g * HALF, (g + 1) * HALF)
@@ -168,7 +174,7 @@ def tile_self_attn_pa_t_kernel(tc, x, q_w, q_b, k_w, k_b, a_h, a_w, out_0, out_1
                     out=k_sb[b][:, e, pixels],
                     in0=banks[b, g][e][:],
                     scalar=kb[:, e : e + 1],
-                    in1=gated[b][e][:, pixels],
+                    in1=gated[b][:, e, pixels],
                     op0=ADD,
                     op1=ADD,
                 )
@@ -177,25 +183,23 @@ def tile_self_attn_pa_t_kernel(tc, x, q_w, q_b, k_w, k_b, a_h, a_w, out_0, out_1
             )
             for pair in range(Q_TILES // 2):
                 nc.vector.tensor_tensor(
-                    out=q_sb[b][:, g, 2 * pair : 2 * pair + 2, :], in0=banks[b, g][2 + pair][:], in1=qb[:], op=ADD
+                    out=q_sb[b][:, g, 2 * pair : 2 * pair + 2, :],
+                    in0=banks[b, g][2 + pair][:],
+                    in1=qb[:].unsqueeze(1).to_broadcast([P, 2, D]),
+                    op=ADD,
                 )
             nc.sync.dma_start(out=out_0[b, pixels, :].rearrange("(s m) d -> m s d", m=P), in_=q_sb[b][:, g])
 
+        gate_at_once(0)
+        kw_codes, kw_scales = quantise_weight(nc, const, psum, ident, kw_rows, "kw")
+        qw_codes, qw_scales = quantise_weight(nc, const, psum, ident, qw_rows, "qw")
         prepare(0)
-        prepare(1)
-        quantise(0)
-        for g in range(HALVES):
-            project(0, g)
-        kb = const.tile([P, 2], F32)
-        nc.vector.tensor_copy(out=kb[:], in_=kb_bf[:])
-        qb = const.tile([P, 2, D], F32)
-        nc.vector.tensor_copy(out=qb[:], in_=qb_bf[:].unsqueeze(1).to_broadcast([P, 2, D]))
         for b in range(B):
-            if b + 2 < B:
-                prepare(b + 2)
+            quantise(b)
             if b + 1 < B:
-                quantise(b + 1)
+                gate_by_rows(b + 1)
+                prepare(b + 1)
+            for g in range(HALVES):
+                project(b, g)
             for g in range(HALVES):
                 finish(b, g)
-                if b + 1 < B:
-                    project(b + 1, g)

@@ -54,21 +54,17 @@ def tile_self_attn_pa_t_kernel(tc, x, q_w, q_b, k_w, k_b, a_h, a_w, out_0, out_1
         ctx.enter_context(tc.manual_schedule())
 
         x_tiles = [maps.tile([P, PACK, N], BF16, name="x_b") for b in range(B)]
+        ah = const.tile([P, B, 2, HH], BF16)
+        aw = const.tile([P, B, 2, WW], BF16)
 
         def load_map(b):
+            nc.sync.dma_start(out=ah[:, b], in_=a_h[b].rearrange("(p e) i -> p e i", e=2))
+            nc.sync.dma_start(out=aw[:, b], in_=a_w[b].rearrange("(p e) j -> p e j", e=2))
             nc.sync.dma_start(
                 out=x_tiles[b][:].rearrange("p (u e) n -> p u (e n)", u=2),
                 in_=x[b].rearrange("(u p e) i j -> p u (e i j)", u=2, e=2),
             )
 
-        ah = const.tile([P, B, 2, HH], BF16)
-        nc.sync.dma_start(
-            out=ah[:].rearrange("p b e i -> p b (e i)"), in_=a_h.rearrange("b (p e) i -> p b (e i)", e=2)
-        )
-        aw = const.tile([P, B, 2, WW], BF16)
-        nc.sync.dma_start(
-            out=aw[:].rearrange("p b e j -> p b (e j)"), in_=a_w.rearrange("b (p e) j -> p b (e j)", e=2)
-        )
         load_map(0)
         kw_rows = const.tile([P, 2, C], BF16)
         nc.sync.dma_start(out=kw_rows[:], in_=k_w.rearrange("(p e) c -> p e c", e=2))
@@ -76,7 +72,6 @@ def tile_self_attn_pa_t_kernel(tc, x, q_w, q_b, k_w, k_b, a_h, a_w, out_0, out_1
         nc.sync.dma_start(out=qw_rows[:], in_=q_w.rearrange("(h p) c -> p h c", p=P))
         for b in range(1, B):
             load_map(b)
-
         kb = const.tile([P, 2], BF16)
         nc.scalar.dma_start(out=kb[:], in_=k_b.rearrange("(p e) -> p e", e=2))
         qb = const.tile([P, D], BF16)
@@ -85,7 +80,6 @@ def tile_self_attn_pa_t_kernel(tc, x, q_w, q_b, k_w, k_b, a_h, a_w, out_0, out_1
         ident = const.tile([P, P], F32)
         make_identity(nc, ident[:])
         ah_f32 = const.tile([P, B, 2, HH], F32)
-        nc.vector.tensor_copy(out=ah_f32[:], in_=ah[:])
 
         grouped, gated, codes, scales, banks, q_sb, k_sb = {}, {}, {}, {}, {}, {}, {}
 
@@ -100,6 +94,7 @@ def tile_self_attn_pa_t_kernel(tc, x, q_w, q_b, k_w, k_b, a_h, a_w, out_0, out_1
 
         def gate_by_rows(b):
             gated[b] = gates.tile([P, 2, N], F32, name="gated")
+            nc.scalar.copy(out=ah_f32[:, b], in_=ah[:, b])
             for e in range(2):
                 for i in range(HH):
                     nc.scalar.activation(
@@ -109,7 +104,7 @@ def tile_self_attn_pa_t_kernel(tc, x, q_w, q_b, k_w, k_b, a_h, a_w, out_0, out_1
                         scale=ah_f32[:, b, e, i : i + 1],
                     )
 
-        def prepare(b):
+        def prepare(b, scalar_pixels):
             x_b = x_tiles[b]
             for g in range(HALVES):
                 pixels = slice(g * HALF, (g + 1) * HALF)
@@ -119,12 +114,12 @@ def tile_self_attn_pa_t_kernel(tc, x, q_w, q_b, k_w, k_b, a_h, a_w, out_0, out_1
                     )
             grouped[b] = work.tile([P, N, PACK], BF16, align_bytes=64, name="grouped")
             nc.scalar.copy(
-                out=grouped[b][:, :SCALAR_PIXELS].rearrange("p (c i) t -> p c t i", i=RUN),
-                in_=x_b[:, :, :SCALAR_PIXELS].rearrange("p t (c i) -> p c t i", i=RUN),
+                out=grouped[b][:, :scalar_pixels].rearrange("p (c i) t -> p c t i", i=RUN),
+                in_=x_b[:, :, :scalar_pixels].rearrange("p t (c i) -> p c t i", i=RUN),
             )
             nc.vector.tensor_copy(
-                out=grouped[b][:, SCALAR_PIXELS:].rearrange("p (c i) t -> p c t i", i=RUN),
-                in_=x_b[:, :, SCALAR_PIXELS:].rearrange("p t (c i) -> p c t i", i=RUN),
+                out=grouped[b][:, scalar_pixels:].rearrange("p (c i) t -> p c t i", i=RUN),
+                in_=x_b[:, :, scalar_pixels:].rearrange("p t (c i) -> p c t i", i=RUN),
             )
 
         def quantise(b):
@@ -193,12 +188,12 @@ def tile_self_attn_pa_t_kernel(tc, x, q_w, q_b, k_w, k_b, a_h, a_w, out_0, out_1
         gate_at_once(0)
         kw_codes, kw_scales = quantise_weight(nc, const, psum, ident, kw_rows, "kw")
         qw_codes, qw_scales = quantise_weight(nc, const, psum, ident, qw_rows, "qw")
-        prepare(0)
+        prepare(0, N // 2)
         for b in range(B):
             quantise(b)
             if b + 1 < B:
                 gate_by_rows(b + 1)
-                prepare(b + 1)
+                prepare(b + 1, SCALAR_PIXELS)
             for g in range(HALVES):
                 project(b, g)
             for g in range(HALVES):

@@ -20,7 +20,7 @@ HALF = 512
 Q_TILES = HALF // P
 RUN = 4
 HALVES = N // HALF
-SCALAR_PIXELS = 3 * N // 4
+SCALAR_PIXELS = N // 2
 
 FLOPS = 2 * 2 * B * D * C * N
 
@@ -104,7 +104,7 @@ def tile_self_attn_pa_t_kernel(tc, x, q_w, q_b, k_w, k_b, a_h, a_w, out_0, out_1
                         scale=ah_f32[:, b, e, i : i + 1],
                     )
 
-        def prepare(b, scalar_pixels):
+        def prepare(b):
             x_b = x_tiles[b]
             for g in range(HALVES):
                 pixels = slice(g * HALF, (g + 1) * HALF)
@@ -114,12 +114,12 @@ def tile_self_attn_pa_t_kernel(tc, x, q_w, q_b, k_w, k_b, a_h, a_w, out_0, out_1
                     )
             grouped[b] = work.tile([P, N, PACK], BF16, align_bytes=64, name="grouped")
             nc.scalar.copy(
-                out=grouped[b][:, :scalar_pixels].rearrange("p (c i) t -> p c t i", i=RUN),
-                in_=x_b[:, :, :scalar_pixels].rearrange("p t (c i) -> p c t i", i=RUN),
+                out=grouped[b][:, :SCALAR_PIXELS].rearrange("p (c i) t -> p c t i", i=RUN),
+                in_=x_b[:, :, :SCALAR_PIXELS].rearrange("p t (c i) -> p c t i", i=RUN),
             )
             nc.vector.tensor_copy(
-                out=grouped[b][:, scalar_pixels:].rearrange("p (c i) t -> p c t i", i=RUN),
-                in_=x_b[:, :, scalar_pixels:].rearrange("p t (c i) -> p c t i", i=RUN),
+                out=grouped[b][:, SCALAR_PIXELS:].rearrange("p (c i) t -> p c t i", i=RUN),
+                in_=x_b[:, :, SCALAR_PIXELS:].rearrange("p t (c i) -> p c t i", i=RUN),
             )
 
         def quantise(b):
@@ -188,12 +188,12 @@ def tile_self_attn_pa_t_kernel(tc, x, q_w, q_b, k_w, k_b, a_h, a_w, out_0, out_1
         gate_at_once(0)
         kw_codes, kw_scales = quantise_weight(nc, const, psum, ident, kw_rows, "kw")
         qw_codes, qw_scales = quantise_weight(nc, const, psum, ident, qw_rows, "qw")
-        prepare(0, N // 2)
+        prepare(0)
         for b in range(B):
             quantise(b)
             if b + 1 < B:
                 gate_by_rows(b + 1)
-                prepare(b + 1, SCALAR_PIXELS)
+                prepare(b + 1)
             for g in range(HALVES):
                 project(b, g)
             for g in range(HALVES):

from contextlib import ExitStack

import concourse.mybir as mybir
from concourse.masks import make_identity

F32 = mybir.dt.float32
BF16 = mybir.dt.bfloat16
U32 = mybir.dt.uint32
U8 = mybir.dt.uint8
FP8X4 = mybir.dt.float8_e4m3fn_x4
ADD = mybir.AluOpType.add
MULT = mybir.AluOpType.mult
COPY = mybir.ActivationFunctionType.Copy

B, C, D, HH, WW = 8, 512, 256, 32, 32
N = HH * WW
P = 128
PACK = 4
HALF = 512
Q_TILES = HALF // P
RUN = 4
HALVES = N // HALF
SCALAR_PIXELS = N // 2

FLOPS = 2 * 2 * B * D * C * N


def quantise_weight(nc, const, psum, ident, rows, label):
    turned = psum.tile([P, 2, D], F32, tag="bank", name=label + "_turned")
    for h in range(2):
        words = rows[:, h, :].bitcast(F32)
        for u in range(2):
            nc.tensor.transpose(turned[:, u, h * P : (h + 1) * P], words[:, u * P : (u + 1) * P], ident[:])
    grouped = const.tile([P, D * PACK], BF16, align_bytes=64, name=label + "_grouped")
    nc.vector.tensor_copy(
        out=grouped[:].bitcast(F32).rearrange("p (c u) -> p c u", u=2),
        in_=turned[:].rearrange("p u c -> p c u"),
    )
    codes = const.tile([P, D], U32, align_bytes=64, name=label + "_codes")
    scales = const.tile([P, D], U8, align_bytes=64, name=label + "_scales")
    nc.vector.quantize_mx(out=codes[:].bitcast(FP8X4), scales=scales[:], in_=grouped[:])
    return codes, scales


def tile_self_attn_pa_t_kernel(tc, x, q_w, q_b, k_w, k_b, a_h, a_w, out_0, out_1):
    nc = tc.nc
    with ExitStack() as ctx:
        const = ctx.enter_context(tc.tile_pool(name="const", bufs=1))
        maps = ctx.enter_context(tc.tile_pool(name="maps", bufs=B))
        work = ctx.enter_context(tc.tile_pool(name="work", bufs=2))
        gates = ctx.enter_context(tc.tile_pool(name="gates", bufs=3))
        results = ctx.enter_context(tc.tile_pool(name="results", bufs=3))
        psum = ctx.enter_context(tc.psum_pool(name="psum", bufs=8))
        ctx.enter_context(tc.manual_schedule())

        x_tiles = [maps.tile([P, PACK, N], BF16, name="x_b") for b in range(B)]
        ah = const.tile([P, B, 2, HH], BF16)
        aw = const.tile([P, B, 2, WW], BF16)

        def load_map(b):
            nc.sync.dma_start(out=ah[:, b], in_=a_h[b].rearrange("(p e) i -> p e i", e=2))
            nc.sync.dma_start(out=aw[:, b], in_=a_w[b].rearrange("(p e) j -> p e j", e=2))
            nc.sync.dma_start(
                out=x_tiles[b][:].rearrange("p (u e) n -> p u (e n)", u=2),
                in_=x[b].rearrange("(u p e) i j -> p u (e i j)", u=2, e=2),
            )

        load_map(0)
        kw_rows = const.tile([P, 2, C], BF16)
        nc.sync.dma_start(out=kw_rows[:], in_=k_w.rearrange("(p e) c -> p e c", e=2))
        qw_rows = const.tile([P, 2, C], BF16)
        nc.sync.dma_start(out=qw_rows[:], in_=q_w.rearrange("(h p) c -> p h c", p=P))
        for b in range(1, B):
            load_map(b)
        kb = const.tile([P, 2], BF16)
        nc.scalar.dma_start(out=kb[:], in_=k_b.rearrange("(p e) -> p e", e=2))
        qb = const.tile([P, D], BF16)
        nc.scalar.dma_start(out=qb[:], in_=q_b.partition_broadcast(P))

        ident = const.tile([P, P], F32)
        make_identity(nc, ident[:])
        ah_f32 = const.tile([P, B, 2, HH], F32)

        grouped, gated, codes, scales, banks, q_sb, k_sb = {}, {}, {}, {}, {}, {}, {}

        def gate_at_once(b):
            gated[b] = gates.tile([P, 2, N], F32, name="gated")
            nc.vector.tensor_tensor(
                out=gated[b][:].rearrange("p e (i j) -> p e i j", j=WW),
                in0=ah[:, b].unsqueeze(3).to_broadcast([P, 2, HH, WW]),
                in1=aw[:, b].unsqueeze(2).to_broadcast([P, 2, HH, WW]),
                op=MULT,
            )

        def gate_by_rows(b):
            gated[b] = gates.tile([P, 2, N], F32, name="gated")
            nc.scalar.copy(out=ah_f32[:, b], in_=ah[:, b])
            for e in range(2):
                for i in range(HH):
                    nc.scalar.activation(
                        out=gated[b][:, e, i * WW : (i + 1) * WW],
                        in_=aw[:, b, e, :],
                        func=COPY,
                        scale=ah_f32[:, b, e, i : i + 1],
                    )

        def prepare(b):
            x_b = x_tiles[b]
            for g in range(HALVES):
                pixels = slice(g * HALF, (g + 1) * HALF)
                for e in range(2):
                    nc.gpsimd.tensor_tensor(
                        out=gated[b][:, e, pixels], in0=gated[b][:, e, pixels], in1=x_b[:, e, pixels], op=MULT
                    )
            grouped[b] = work.tile([P, N, PACK], BF16, align_bytes=64, name="grouped")
            nc.scalar.copy(
                out=grouped[b][:, :SCALAR_PIXELS].rearrange("p (c i) t -> p c t i", i=RUN),
                in_=x_b[:, :, :SCALAR_PIXELS].rearrange("p t (c i) -> p c t i", i=RUN),
            )
            nc.vector.tensor_copy(
                out=grouped[b][:, SCALAR_PIXELS:].rearrange("p (c i) t -> p c t i", i=RUN),
                in_=x_b[:, :, SCALAR_PIXELS:].rearrange("p t (c i) -> p c t i", i=RUN),
            )

        def quantise(b):
            codes[b] = work.tile([P, N], U32, align_bytes=64, name="codes")
            scales[b] = work.tile([P, N], U8, align_bytes=64, name="scales")
            nc.vector.quantize_mx(
                out=codes[b][:].bitcast(FP8X4), scales=scales[b][:], in_=grouped[b][:].rearrange("p n t -> p (n t)")
            )

        def project(b, g):
            pixels = slice(g * HALF, (g + 1) * HALF)
            banks[b, g] = []
            for e in range(2):
                k_acc = psum.tile([P, HALF], F32, tag="bank")
                nc.tensor.matmul_mx(
                    out=k_acc[:],
                    lhsT=kw_codes[:, e * P : (e + 1) * P].bitcast(FP8X4),
                    lhsT_scale=kw_scales[:, e * P : (e + 1) * P],
                    rhs=codes[b][:, pixels].bitcast(FP8X4),
                    rhs_scale=scales[b][:, pixels],
                    start=True,
                    stop=True,
                )
                banks[b, g].append(k_acc)
            for pair in range(Q_TILES // 2):
                q_acc = psum.tile([P, 2, D], F32, tag="bank")
                for s in range(2):
                    first = g * HALF + (2 * pair + s) * P
                    nc.tensor.matmul_mx(
                        out=q_acc[:, s, :],
                        lhsT=codes[b][:, first : first + P].bitcast(FP8X4),
                        lhsT_scale=scales[b][:, first : first + P],
                        rhs=qw_codes[:].bitcast(FP8X4),
                        rhs_scale=qw_scales[:],
                        start=True,
                        stop=True,
                    )
                banks[b, g].append(q_acc)

        def finish(b, g):
            pixels = slice(g * HALF, (g + 1) * HALF)
            if g == 0:
                q_sb[b] = results.tile([P, HALVES, Q_TILES, D], F32, name="q_sb")
                k_sb[b] = results.tile([P, 2, N], F32, name="k_sb")
            for e in range(2):
                nc.vector.scalar_tensor_tensor(
                    out=k_sb[b][:, e, pixels],
                    in0=banks[b, g][e][:],
                    scalar=kb[:, e : e + 1],
                    in1=gated[b][:, e, pixels],
                    op0=ADD,
                    op1=ADD,
                )
            nc.sync.dma_start(
                out=out_1[b].rearrange("(p e) n -> p e n", e=2)[:, :, pixels], in_=k_sb[b][:, :, pixels]
            )
            for pair in range(Q_TILES // 2):
                nc.vector.tensor_tensor(
                    out=q_sb[b][:, g, 2 * pair : 2 * pair + 2, :],
                    in0=banks[b, g][2 + pair][:],
                    in1=qb[:].unsqueeze(1).to_broadcast([P, 2, D]),
                    op=ADD,
                )
            nc.sync.dma_start(out=out_0[b, pixels, :].rearrange("(s m) d -> m s d", m=P), in_=q_sb[b][:, g])

        gate_at_once(0)
        kw_codes, kw_scales = quantise_weight(nc, const, psum, ident, kw_rows, "kw")
        qw_codes, qw_scales = quantise_weight(nc, const, psum, ident, qw_rows, "qw")
        prepare(0)
        for b in range(B):
            quantise(b)
            if b + 1 < B:
                gate_by_rows(b + 1)
                prepare(b + 1)
            for g in range(HALVES):
                project(b, g)
            for g in range(HALVES):
                finish(b, g)
